import numpy as np
import ml_dtypes


def mxq(x, axis, fmt="e4m3"):
    dtype, down = {"e4m3": (ml_dtypes.float8_e4m3fn, 7), "e5m2": (ml_dtypes.float8_e5m2, 14)}[fmt]
    v = np.moveaxis(np.asarray(x, np.float32).astype(ml_dtypes.bfloat16).astype(np.float64), axis, -1)
    blocks = v.reshape(v.shape[:-1] + (-1, 32))
    amax = np.abs(blocks).max(-1, keepdims=True)
    byte = np.maximum(np.where(amax > 0, np.frexp(amax)[1] - 1 + 127, 0) - down, 1)
    scale = np.exp2(byte - 127.0)
    codes = (blocks / scale).astype(np.float32).astype(dtype).astype(np.float64)
    return np.moveaxis((codes * scale).reshape(v.shape), -1, axis)


WIDE = False


def mx_kscale(k):
    if not WIDE:
        return np.ones(k)
    levels = np.array([10, -10, 5, -5, 0])
    a = np.random.permutation(np.resize(levels, k // 512 * 4)).reshape(k // 512, 4)
    idx = np.arange(k)
    return np.exp2(a[idx // 512, idx % 128 // 32])


BF16 = ml_dtypes.bfloat16


def bf(x):
    return np.asarray(x, np.float32).astype(BF16)


def f64(x):
    return np.asarray(x).astype(np.float64)


E2M1 = np.array([0.0, 0.5, 1.0, 1.5, 2.0, 3.0, 4.0, 6.0, -0.0, -0.5, -1.0, -1.5, -2.0, -3.0, -4.0, -6.0])


def pack_weight(w, fmt):
    k, n = w.shape
    w = f64(bf(w)).reshape(k // 32, 32, n)
    amax = np.abs(w).max(1)
    if fmt == "e4m3":
        byte = np.frexp(amax)[1] - 1 + 127 - 7
    else:
        mant, ex = np.frexp(amax / 6.0)
        byte = np.where(mant > 0.5, ex, ex - 1) + 127
    byte = np.clip(np.where(amax > 0, byte, 1), 1, 254)
    scaled = (w * np.exp2(127.0 - byte)[:, None, :]).reshape(k, n).astype(np.float32)
    by_word = np.ascontiguousarray(scaled.reshape(k // 512, 128, 4, n).transpose(0, 1, 3, 2))
    if fmt == "e4m3":
        words = by_word.astype(ml_dtypes.float8_e4m3fn).view(np.uint8)
    else:
        c = by_word.astype(ml_dtypes.float4_e2m1fn).view(np.uint8) & 0xF
        words = c[..., 0::2] | (c[..., 1::2] << 4)
    return np.ascontiguousarray(words), np.ascontiguousarray(byte.astype(np.uint8).reshape(k // 512, 16, n))


def unpack_weight(words, scales, fmt):
    g, p, n, _ = words.shape
    if fmt == "e4m3":
        vals = np.ascontiguousarray(words).view(ml_dtypes.float8_e4m3fn).astype(np.float64)
    else:
        nib = np.empty((g, p, n, 4), np.uint8)
        nib[..., 0::2] = words & 0xF
        nib[..., 1::2] = words >> 4
        vals = E2M1[nib]
    vals = vals * np.repeat(np.exp2(scales.astype(np.float64) - 127.0), 8, axis=1)[..., None]
    return vals.transpose(0, 1, 3, 2).reshape(g * 512, n)

def pack4(w):
    words, scales = pack_weight(w, "e2m1")
    return words.reshape(words.shape[0], 128, -1), scales


def unpack4(words, scales):
    return unpack_weight(words.reshape(words.shape[0], 128, -1, 2), scales, "e2m1")


N, S, D, H = 8, 512, 512, 4
L = N * S
DH = D // H


def rope(t, cos, sin):
    tr = t[..., 0::2]
    ti = t[..., 1::2]
    c = cos[:, None, :]
    s = sin[:, None, :]
    out_r = tr * c - ti * s
    out_i = tr * s + ti * c
    return np.stack([out_r, out_i], axis=-1).reshape(t.shape)


def setup_inputs():
    s = mx_kscale(D)
    ang = np.random.uniform(0.0, 2.0 * np.pi, (L, DH // 2))
    x = bf(np.random.standard_normal((L, D)) * s)
    words, scales = pack4(np.random.standard_normal((D, 2 * D)) * 1.5 / np.sqrt(D) / s[:, None])
    b_qk = bf(np.random.standard_normal(2 * D) * 0.1)
    return {"x": x,
            "w_qk_words": words, "w_qk_scales": scales,
            "b_qk": b_qk,
            "freqs_cos": bf(np.cos(ang)), "freqs_sin": bf(np.sin(ang))}


def reference(x, w_qk_words, w_qk_scales, b_qk, freqs_cos, freqs_sin):
    qk = (mxq(f64(x), 1, "e4m3") @ unpack4(w_qk_words, w_qk_scales)) + f64(b_qk)
    q, k = [t.reshape(L, H, DH) for t in np.split(qk, 2, axis=-1)]
    c, s = f64(freqs_cos), f64(freqs_sin)
    return rope(q, c, s), rope(k, c, s)

@@ -1,0 +1,195 @@
+from contextlib import ExitStack
+
+import concourse.masks as masks
+import concourse.mybir as mybir
+
+F32 = mybir.dt.float32
+BF16 = mybir.dt.bfloat16
+U8 = mybir.dt.uint8
+U32 = mybir.dt.uint32
+I32 = mybir.dt.int32
+FP8X4 = mybir.dt.float8_e4m3fn_x4
+FP4X4 = mybir.dt.float4_e2m1fn_x4
+MULT = mybir.AluOpType.mult
+ADD = mybir.AluOpType.add
+IDENTITY = mybir.ActivationFunctionType.Identity
+
+P = 128
+PACK = 4
+TOKENS = 4096
+K = P * PACK
+HEADS = 4
+HEAD_DIM = 128
+PAIRS = HEAD_DIM // 2
+HALF = HEADS * HEAD_DIM
+TOKEN_TILES = TOKENS // P
+CHUNK_TILES = 4
+CHUNK_TOKENS = CHUNK_TILES * P
+CHUNKS = TOKEN_TILES // CHUNK_TILES
+SCALE_ROWS = 4
+
+FLOPS = 2 * TOKENS * K * 2 * HALF
+
+
+def tile_moonvitvisiontower_pa_t_kernel(
+    tc, x, w_qk_words, w_qk_scales, b_qk, freqs_cos, freqs_sin, out_0, out_1
+):
+    nc = tc.nc
+    x_rows = x.rearrange("(p g) k -> p g k", g=TOKEN_TILES)
+    out_rows = [
+        out_0.rearrange("(p g) h d -> p g (h d)", g=TOKEN_TILES),
+        out_1.rearrange("(p g) h d -> p g (h d)", g=TOKEN_TILES),
+    ]
+
+    with ExitStack() as ctx:
+        ctx.enter_context(tc.manual_schedule())
+        keep = ctx.enter_context(tc.tile_pool(name="keep", bufs=1))
+        stage = ctx.enter_context(tc.tile_pool(name="stage", bufs=2))
+        work = ctx.enter_context(tc.tile_pool(name="work", bufs=4))
+        results = ctx.enter_context(tc.tile_pool(name="results", bufs=3))
+        psum_x = ctx.enter_context(tc.psum_pool(name="psum_x", bufs=2))
+        psum_u = ctx.enter_context(tc.psum_pool(name="psum_u", bufs=2))
+        psum_a = ctx.enter_context(tc.psum_pool(name="psum_a", bufs=4))
+
+        x_sb = keep.tile([P, TOKEN_TILES, K], BF16)
+        w_words = keep.tile([P, 2 * 2 * HALF], U8, align_bytes=64)
+        w_scales = keep.tile([P, 2 * HALF], U8, align_bytes=64)
+        bias_rows = keep.tile([P, P], BF16)
+        cos_sb = keep.tile([P, TOKEN_TILES, PAIRS], BF16)
+        sin_sb = keep.tile([P, TOKEN_TILES, PAIRS], BF16)
+        neg_sin = keep.tile([P, TOKEN_TILES, PAIRS], BF16)
+        ident = keep.tile([P, P], F32)
+
+        nc.vector.memset(w_scales[:].bitcast(I32), 0)
+        nc.vector.memset(bias_rows[:], 0.0)
+        masks.make_identity(nc, ident[:])
+
+        def load_x(c):
+            tiles = slice(c * CHUNK_TILES, (c + 1) * CHUNK_TILES)
+            nc.sync.dma_start(out=x_sb[:, tiles, :], in_=x_rows[:, tiles, :])
+
+        load_x(0)
+        nc.sync.dma_start(out=w_words[:].bitcast(I32), in_=w_qk_words[0].bitcast(I32))
+        for quadrant in range(P // 32):
+            nc.sync.dma_start(
+                out=w_scales[32 * quadrant : 32 * quadrant + SCALE_ROWS, :].bitcast(I32),
+                in_=w_qk_scales[
+                    0, SCALE_ROWS * quadrant : SCALE_ROWS * (quadrant + 1), :
+                ].bitcast(I32),
+            )
+        nc.sync.dma_start(
+            out=bias_rows[0 : 2 * HEADS, :], in_=b_qk.rearrange("(r n) -> r n", n=HEAD_DIM)
+        )
+        nc.sync.dma_start(
+            out=cos_sb[:], in_=freqs_cos.rearrange("(p g) j -> p g j", g=TOKEN_TILES)
+        )
+        nc.sync.dma_start(
+            out=sin_sb[:], in_=freqs_sin.rearrange("(p g) j -> p g j", g=TOKEN_TILES)
+        )
+        for c in range(1, CHUNKS):
+            load_x(c)
+
+        nc.gpsimd.tensor_scalar(
+            out=neg_sin[:], in0=sin_sb[:], scalar1=-1.0, scalar2=0.0, op0=MULT, op1=ADD
+        )
+
+        def quantise_chunk(c):
+            grouped = stage.tile([P, CHUNK_TOKENS * PACK], BF16, align_bytes=64)
+            grouped_words = grouped[:].bitcast(F32).rearrange(
+                "p (t m u) -> p t m u", t=CHUNK_TILES, u=2
+            )
+            for first in range(0, CHUNK_TILES, 2):
+                x_t = psum_x.tile([P, 2, 2, P], F32, tag="x_t")
+                for i in range(2):
+                    words = x_sb[:, c * CHUNK_TILES + first + i, :].bitcast(F32)
+                    for u in range(2):
+                        nc.tensor.transpose(x_t[:, i, u, :], words[:, u : K // 2 : 2], ident[:])
+                nc.scalar.copy(
+                    out=grouped_words[:, first : first + 2, :, :],
+                    in_=x_t[:].rearrange("p i u m -> p i m u"),
+                )
+            x_codes = stage.tile([P, CHUNK_TOKENS], U32, align_bytes=64)
+            x_scales = stage.tile([P, CHUNK_TOKENS], U8, align_bytes=64)
+            nc.vector.quantize_mx(
+                out=x_codes[:].bitcast(FP8X4), scales=x_scales[:], in_=grouped[:]
+            )
+            return x_codes, x_scales
+
+        bias_rows_f32 = keep.tile([P, P], F32)
+        nc.vector.tensor_copy(out=bias_rows_f32[:], in_=bias_rows[:])
+        operand = quantise_chunk(0)
+        bias_t = psum_x.tile([P, P], F32, tag="x_t")
+        nc.tensor.transpose(bias_t[:], bias_rows_f32[:], ident[:])
+        bias_col = keep.tile([P, 2 * HEADS], F32)
+        nc.vector.tensor_copy(out=bias_col[:], in_=bias_t[:, 0 : 2 * HEADS])
+
+        def project_and_rotate(c, half, x_codes, x_scales):
+            sums_t = stage.tile([P, HEADS, CHUNK_TOKENS], F32)
+            for h in range(HEADS):
+                head = half * HEADS + h
+                cols = slice(head * HEAD_DIM, (head + 1) * HEAD_DIM)
+                col_bytes = slice(2 * head * HEAD_DIM, 2 * (head + 1) * HEAD_DIM)
+                product_t = psum_u.tile([P, CHUNK_TOKENS], F32)
+                nc.tensor.matmul_mx(
+                    out=product_t[:],
+                    lhsT=w_words[:, col_bytes].bitcast(FP4X4),
+                    lhsT_scale=w_scales[:, cols],
+                    rhs=x_codes[:].bitcast(FP8X4),
+                    rhs_scale=x_scales[:],
+                    start=True,
+                    stop=True,
+                )
+                nc.scalar.activation(
+                    out=sums_t[:, h, :],
+                    in_=product_t[:],
+                    func=IDENTITY,
+                    bias=bias_col[:, head : head + 1],
+                    scale=1.0,
+                )
+
+            rotated = results.tile([P, CHUNK_TILES, HALF], F32)
+            for t in range(CHUNK_TILES):
+                g = c * CHUNK_TILES + t
+                sums = psum_a.tile([P, HALF], F32)
+                for h in range(HEADS):
+                    nc.tensor.transpose(
+                        sums[:, h * HEAD_DIM : (h + 1) * HEAD_DIM],
+                        sums_t[:, h, t * P : (t + 1) * P],
+                        ident[:],
+                    )
+                pairs = sums[:].rearrange("p (h j e) -> p h j e", h=HEADS, e=2)
+                per_head = [P, HEADS, PAIRS]
+                by_cos = work.tile([P, HALF], F32)
+                nc.vector.tensor_tensor(
+                    out=by_cos[:].rearrange("p (h j e) -> p h j e", h=HEADS, e=2),
+                    in0=pairs,
+                    in1=cos_sb[:, g, :].unsqueeze(1).unsqueeze(3).to_broadcast(per_head + [2]),
+                    op=MULT,
+                )
+                by_sin = work.tile([P, 2, HEADS, PAIRS], F32)
+                nc.vector.tensor_tensor(
+                    out=by_sin[:, 0],
+                    in0=pairs[:, :, :, 1],
+                    in1=neg_sin[:, g, :].unsqueeze(1).to_broadcast(per_head),
+                    op=MULT,
+                )
+                nc.vector.tensor_tensor(
+                    out=by_sin[:, 1],
+                    in0=pairs[:, :, :, 0],
+                    in1=sin_sb[:, g, :].unsqueeze(1).to_broadcast(per_head),
+                    op=MULT,
+                )
+                nc.gpsimd.tensor_tensor(
+                    out=rotated[:, t, :].rearrange("p (m e) -> p m e", e=2),
+                    in0=by_cos[:].rearrange("p (m e) -> p m e", e=2),
+                    in1=by_sin[:].rearrange("p e h j -> p (h j) e"),
+                    op=ADD,
+                )
+            tiles = slice(c * CHUNK_TILES, (c + 1) * CHUNK_TILES)
+            nc.sync.dma_start(out=out_rows[half][:, tiles, :], in_=rotated[:])
+
+        for c in range(CHUNKS):
+            project_and_rotate(c, 0, operand[0], operand[1])
+            following = quantise_chunk(c + 1) if c + 1 < CHUNKS else None
+            project_and_rotate(c, 1, operand[0], operand[1])
+            operand = following

@@ -45,7 +45,7 @@ def tile_moonvitvisiontower_pa_t_kernel(
         ctx.enter_context(tc.manual_schedule())
         keep = ctx.enter_context(tc.tile_pool(name="keep", bufs=1))
         stage = ctx.enter_context(tc.tile_pool(name="stage", bufs=2))
-        work = ctx.enter_context(tc.tile_pool(name="work", bufs=4))
+        work = ctx.enter_context(tc.tile_pool(name="work", bufs=3))
         results = ctx.enter_context(tc.tile_pool(name="results", bufs=3))
         psum_x = ctx.enter_context(tc.psum_pool(name="psum_x", bufs=2))
         psum_u = ctx.enter_context(tc.psum_pool(name="psum_u", bufs=2))
@@ -147,7 +147,8 @@ def tile_moonvitvisiontower_pa_t_kernel(
                     scale=1.0,
                 )
 
-            rotated = results.tile([P, CHUNK_TILES, HALF], F32)
+            by_cos = work.tile([P, CHUNK_TILES, HALF], F32)
+            by_sin = work.tile([P, CHUNK_TILES, 2, HEADS, PAIRS], F32)
             for t in range(CHUNK_TILES):
                 g = c * CHUNK_TILES + t
                 sums = psum_a.tile([P, HALF], F32)
@@ -159,32 +160,31 @@ def tile_moonvitvisiontower_pa_t_kernel(
                     )
                 pairs = sums[:].rearrange("p (h j e) -> p h j e", h=HEADS, e=2)
                 per_head = [P, HEADS, PAIRS]
-                by_cos = work.tile([P, HALF], F32)
                 nc.vector.tensor_tensor(
-                    out=by_cos[:].rearrange("p (h j e) -> p h j e", h=HEADS, e=2),
+                    out=by_cos[:, t, :].rearrange("p (h j e) -> p h j e", h=HEADS, e=2),
                     in0=pairs,
                     in1=cos_sb[:, g, :].unsqueeze(1).unsqueeze(3).to_broadcast(per_head + [2]),
                     op=MULT,
                 )
-                by_sin = work.tile([P, 2, HEADS, PAIRS], F32)
                 nc.vector.tensor_tensor(
-                    out=by_sin[:, 0],
+                    out=by_sin[:, t, 0],
                     in0=pairs[:, :, :, 1],
                     in1=neg_sin[:, g, :].unsqueeze(1).to_broadcast(per_head),
                     op=MULT,
                 )
                 nc.vector.tensor_tensor(
-                    out=by_sin[:, 1],
+                    out=by_sin[:, t, 1],
                     in0=pairs[:, :, :, 0],
                     in1=sin_sb[:, g, :].unsqueeze(1).to_broadcast(per_head),
                     op=MULT,
                 )
-                nc.gpsimd.tensor_tensor(
-                    out=rotated[:, t, :].rearrange("p (m e) -> p m e", e=2),
-                    in0=by_cos[:].rearrange("p (m e) -> p m e", e=2),
-                    in1=by_sin[:].rearrange("p e h j -> p (h j) e"),
-                    op=ADD,
-                )
+            rotated = results.tile([P, CHUNK_TILES, HALF], F32)
+            nc.gpsimd.tensor_tensor(
+                out=rotated[:].rearrange("p t (m e) -> p t m e", e=2),
+                in0=by_cos[:].rearrange("p t (m e) -> p t m e", e=2),
+                in1=by_sin[:].rearrange("p t e h j -> p t (h j) e"),
+                op=ADD,
+            )
             tiles = slice(c * CHUNK_TILES, (c + 1) * CHUNK_TILES)
             nc.sync.dma_start(out=out_rows[half][:, tiles, :], in_=rotated[:])
 

@@ -12,7 +12,7 @@ FP8X4 = mybir.dt.float8_e4m3fn_x4
 FP4X4 = mybir.dt.float4_e2m1fn_x4
 MULT = mybir.AluOpType.mult
 ADD = mybir.AluOpType.add
-IDENTITY = mybir.ActivationFunctionType.Identity
+COPY = mybir.ActivationFunctionType.Copy
 
 P = 128
 PACK = 4
@@ -27,6 +27,7 @@ CHUNK_TILES = 4
 CHUNK_TOKENS = CHUNK_TILES * P
 CHUNKS = TOKEN_TILES // CHUNK_TILES
 SCALE_ROWS = 4
+SIGN = 2 * HEADS
 
 FLOPS = 2 * TOKENS * K * 2 * HALF
 
@@ -36,6 +37,8 @@ def tile_moonvitvisiontower_pa_t_kernel(
 ):
     nc = tc.nc
     x_rows = x.rearrange("(p g) k -> p g k", g=TOKEN_TILES)
+    cos_rows = freqs_cos.rearrange("(p g) j -> p g j", g=TOKEN_TILES)
+    sin_rows = freqs_sin.rearrange("(p g) j -> p g j", g=TOKEN_TILES)
     out_rows = [
         out_0.rearrange("(p g) h d -> p g (h d)", g=TOKEN_TILES),
         out_1.rearrange("(p g) h d -> p g (h d)", g=TOKEN_TILES),
@@ -45,30 +48,36 @@ def tile_moonvitvisiontower_pa_t_kernel(
         ctx.enter_context(tc.manual_schedule())
         keep = ctx.enter_context(tc.tile_pool(name="keep", bufs=1))
         stage = ctx.enter_context(tc.tile_pool(name="stage", bufs=2))
-        work = ctx.enter_context(tc.tile_pool(name="work", bufs=3))
+        products = ctx.enter_context(tc.tile_pool(name="products", bufs=3))
         results = ctx.enter_context(tc.tile_pool(name="results", bufs=3))
-        psum_x = ctx.enter_context(tc.psum_pool(name="psum_x", bufs=2))
-        psum_u = ctx.enter_context(tc.psum_pool(name="psum_u", bufs=2))
-        psum_a = ctx.enter_context(tc.psum_pool(name="psum_a", bufs=4))
+        psum_prep = ctx.enter_context(tc.psum_pool(name="psum_prep", bufs=2))
+        psum_mx = ctx.enter_context(tc.psum_pool(name="psum_mx", bufs=4))
+        psum_out = ctx.enter_context(tc.psum_pool(name="psum_out", bufs=2))
 
         x_sb = keep.tile([P, TOKEN_TILES, K], BF16)
-        w_words = keep.tile([P, 2 * 2 * HALF], U8, align_bytes=64)
-        w_scales = keep.tile([P, 2 * HALF], U8, align_bytes=64)
-        bias_rows = keep.tile([P, P], BF16)
         cos_sb = keep.tile([P, TOKEN_TILES, PAIRS], BF16)
         sin_sb = keep.tile([P, TOKEN_TILES, PAIRS], BF16)
-        neg_sin = keep.tile([P, TOKEN_TILES, PAIRS], BF16)
+        w_words = keep.tile([P, 2 * 2 * HALF], U8, align_bytes=64)
+        w_scales = keep.tile([P, 2 * HALF], U8, align_bytes=64)
+        const_rows = keep.tile([P, P], BF16)
         ident = keep.tile([P, P], F32)
+        swap = keep.tile([P, P], F32)
 
         nc.vector.memset(w_scales[:].bitcast(I32), 0)
-        nc.vector.memset(bias_rows[:], 0.0)
+        nc.vector.memset(const_rows[:, 0:P:2], 1.0)
+        nc.vector.memset(const_rows[:, 1:P:2], -1.0)
         masks.make_identity(nc, ident[:])
 
-        def load_x(c):
+        def load_chunk(c):
             tiles = slice(c * CHUNK_TILES, (c + 1) * CHUNK_TILES)
             nc.sync.dma_start(out=x_sb[:, tiles, :], in_=x_rows[:, tiles, :])
+            nc.sync.dma_start(out=cos_sb[:, tiles, :], in_=cos_rows[:, tiles, :])
+            nc.sync.dma_start(out=sin_sb[:, tiles, :], in_=sin_rows[:, tiles, :])
 
-        load_x(0)
+        nc.sync.dma_start(
+            out=const_rows[0 : 2 * HEADS, :], in_=b_qk.rearrange("(r n) -> r n", n=HEAD_DIM)
+        )
+        load_chunk(0)
         nc.sync.dma_start(out=w_words[:].bitcast(I32), in_=w_qk_words[0].bitcast(I32))
         for quadrant in range(P // 32):
             nc.sync.dma_start(
@@ -77,29 +86,28 @@ def tile_moonvitvisiontower_pa_t_kernel(
                     0, SCALE_ROWS * quadrant : SCALE_ROWS * (quadrant + 1), :
                 ].bitcast(I32),
             )
-        nc.sync.dma_start(
-            out=bias_rows[0 : 2 * HEADS, :], in_=b_qk.rearrange("(r n) -> r n", n=HEAD_DIM)
-        )
-        nc.sync.dma_start(
-            out=cos_sb[:], in_=freqs_cos.rearrange("(p g) j -> p g j", g=TOKEN_TILES)
-        )
-        nc.sync.dma_start(
-            out=sin_sb[:], in_=freqs_sin.rearrange("(p g) j -> p g j", g=TOKEN_TILES)
-        )
         for c in range(1, CHUNKS):
-            load_x(c)
+            load_chunk(c)
 
-        nc.gpsimd.tensor_scalar(
-            out=neg_sin[:], in0=sin_sb[:], scalar1=-1.0, scalar2=0.0, op0=MULT, op1=ADD
-        )
+        ident_pairs = ident[:].rearrange("p (j e) -> p j e", e=2)
+        swap_pairs = swap[:].rearrange("p (j e) -> p j e", e=2)
+        nc.vector.tensor_copy(out=swap_pairs[:, :, 0], in_=ident_pairs[:, :, 1])
+        nc.vector.tensor_copy(out=swap_pairs[:, :, 1], in_=ident_pairs[:, :, 0])
 
-        def quantise_chunk(c):
+        const_rows_f32 = keep.tile([P, P], F32)
+        nc.vector.tensor_copy(out=const_rows_f32[:], in_=const_rows[:])
+        consts_ps = psum_prep.tile([P, P], F32, tag="prep")
+        nc.tensor.transpose(consts_ps[:], const_rows_f32[:], ident[:])
+        consts = keep.tile([P, SIGN + 1], F32)
+        nc.vector.tensor_copy(out=consts[:], in_=consts_ps[:, 0 : SIGN + 1])
+
+        def prepare_chunk(c):
             grouped = stage.tile([P, CHUNK_TOKENS * PACK], BF16, align_bytes=64)
             grouped_words = grouped[:].bitcast(F32).rearrange(
                 "p (t m u) -> p t m u", t=CHUNK_TILES, u=2
             )
             for first in range(0, CHUNK_TILES, 2):
-                x_t = psum_x.tile([P, 2, 2, P], F32, tag="x_t")
+                x_t = psum_prep.tile([P, 2, 2, P], F32, tag="prep")
                 for i in range(2):
                     words = x_sb[:, c * CHUNK_TILES + first + i, :].bitcast(F32)
                     for u in range(2):
@@ -108,30 +116,58 @@ def tile_moonvitvisiontower_pa_t_kernel(
                     out=grouped_words[:, first : first + 2, :, :],
                     in_=x_t[:].rearrange("p i u m -> p i m u"),
                 )
+
+            tiles = slice(c * CHUNK_TILES, (c + 1) * CHUNK_TILES)
+            wide = [P, CHUNK_TILES, PAIRS, 2]
+            cos_wide = stage.tile(wide, F32)
+            sin_wide = stage.tile(wide, F32)
+            for doubled, single in ((cos_wide, cos_sb), (sin_wide, sin_sb)):
+                nc.gpsimd.tensor_scalar(
+                    out=doubled[:],
+                    in0=single[:, tiles, :].unsqueeze(3).to_broadcast(wide),
+                    scalar1=1.0,
+                    scalar2=0.0,
+                    op0=MULT,
+                    op1=ADD,
+                )
+            cos_ps = psum_prep.tile([P, CHUNK_TOKENS], F32, tag="prep")
+            for t in range(CHUNK_TILES):
+                nc.tensor.transpose(
+                    cos_ps[:, t * P : (t + 1) * P],
+                    cos_wide[:, t].rearrange("p j e -> p (j e)"),
+                    ident[:],
+                )
+            cos_t = stage.tile([P, CHUNK_TOKENS], F32)
+            nc.scalar.copy(out=cos_t[:], in_=cos_ps[:])
+            sin_ps = psum_prep.tile([P, CHUNK_TOKENS], F32, tag="prep")
+            for t in range(CHUNK_TILES):
+                nc.tensor.transpose(
+                    sin_ps[:, t * P : (t + 1) * P],
+                    sin_wide[:, t].rearrange("p j e -> p (j e)"),
+                    ident[:],
+                )
+            sin_t = stage.tile([P, CHUNK_TOKENS], F32)
+            nc.scalar.activation(
+                out=sin_t[:], in_=sin_ps[:], func=COPY, scale=consts[:, SIGN : SIGN + 1]
+            )
+
             x_codes = stage.tile([P, CHUNK_TOKENS], U32, align_bytes=64)
             x_scales = stage.tile([P, CHUNK_TOKENS], U8, align_bytes=64)
             nc.vector.quantize_mx(
                 out=x_codes[:].bitcast(FP8X4), scales=x_scales[:], in_=grouped[:]
             )
-            return x_codes, x_scales
+            return x_codes, x_scales, cos_t, sin_t
 
-        bias_rows_f32 = keep.tile([P, P], F32)
-        nc.vector.tensor_copy(out=bias_rows_f32[:], in_=bias_rows[:])
-        operand = quantise_chunk(0)
-        bias_t = psum_x.tile([P, P], F32, tag="x_t")
-        nc.tensor.transpose(bias_t[:], bias_rows_f32[:], ident[:])
-        bias_col = keep.tile([P, 2 * HEADS], F32)
-        nc.vector.tensor_copy(out=bias_col[:], in_=bias_t[:, 0 : 2 * HEADS])
-
-        def project_and_rotate(c, half, x_codes, x_scales):
-            sums_t = stage.tile([P, HEADS, CHUNK_TOKENS], F32)
+        def multiply(half, x_codes, x_scales, cos_t, sin_t):
+            by_cos = products.tile([P, HEADS, CHUNK_TOKENS], F32)
+            by_sin = products.tile([P, HEADS, CHUNK_TOKENS], F32)
             for h in range(HEADS):
                 head = half * HEADS + h
                 cols = slice(head * HEAD_DIM, (head + 1) * HEAD_DIM)
                 col_bytes = slice(2 * head * HEAD_DIM, 2 * (head + 1) * HEAD_DIM)
-                product_t = psum_u.tile([P, CHUNK_TOKENS], F32)
+                product = psum_mx.tile([P, CHUNK_TOKENS], F32)
                 nc.tensor.matmul_mx(
-                    out=product_t[:],
+                    out=product[:],
                     lhsT=w_words[:, col_bytes].bitcast(FP4X4),
                     lhsT_scale=w_scales[:, cols],
                     rhs=x_codes[:].bitcast(FP8X4),
@@ -139,57 +175,53 @@ def tile_moonvitvisiontower_pa_t_kernel(
                     start=True,
                     stop=True,
                 )
-                nc.scalar.activation(
-                    out=sums_t[:, h, :],
-                    in_=product_t[:],
-                    func=IDENTITY,
-                    bias=bias_col[:, head : head + 1],
-                    scale=1.0,
-                )
-
-            by_cos = work.tile([P, CHUNK_TILES, HALF], F32)
-            by_sin = work.tile([P, CHUNK_TILES, 2, HEADS, PAIRS], F32)
-            for t in range(CHUNK_TILES):
-                g = c * CHUNK_TILES + t
-                sums = psum_a.tile([P, HALF], F32)
-                for h in range(HEADS):
-                    nc.tensor.transpose(
-                        sums[:, h * HEAD_DIM : (h + 1) * HEAD_DIM],
-                        sums_t[:, h, t * P : (t + 1) * P],
-                        ident[:],
+                for scaled, table in ((by_cos, cos_t), (by_sin, sin_t)):
+                    nc.vector.scalar_tensor_tensor(
+                        out=scaled[:, h, :],
+                        in0=product[:],
+                        scalar=consts[:, head : head + 1],
+                        in1=table[:],
+                        op0=ADD,
+                        op1=MULT,
                     )
-                pairs = sums[:].rearrange("p (h j e) -> p h j e", h=HEADS, e=2)
-                per_head = [P, HEADS, PAIRS]
-                nc.vector.tensor_tensor(
-                    out=by_cos[:, t, :].rearrange("p (h j e) -> p h j e", h=HEADS, e=2),
-                    in0=pairs,
-                    in1=cos_sb[:, g, :].unsqueeze(1).unsqueeze(3).to_broadcast(per_head + [2]),
-                    op=MULT,
-                )
-                nc.vector.tensor_tensor(
-                    out=by_sin[:, t, 0],
-                    in0=pairs[:, :, :, 1],
-                    in1=neg_sin[:, g, :].unsqueeze(1).to_broadcast(per_head),
-                    op=MULT,
-                )
-                nc.vector.tensor_tensor(
-                    out=by_sin[:, t, 1],
-                    in0=pairs[:, :, :, 0],
-                    in1=sin_sb[:, g, :].unsqueeze(1).to_broadcast(per_head),
-                    op=MULT,
-                )
+            return by_cos, by_sin
+
+        def turn_back(c, half, by_cos, by_sin):
             rotated = results.tile([P, CHUNK_TILES, HALF], F32)
-            nc.gpsimd.tensor_tensor(
-                out=rotated[:].rearrange("p t (m e) -> p t m e", e=2),
-                in0=by_cos[:].rearrange("p t (m e) -> p t m e", e=2),
-                in1=by_sin[:].rearrange("p t e h j -> p t (h j) e"),
-                op=ADD,
-            )
+            for t in range(CHUNK_TILES):
+                tokens = slice(t * P, (t + 1) * P)
+                turned = psum_out.tile([P, HALF], F32)
+                for h in range(HEADS):
+                    cols = slice(h * HEAD_DIM, (h + 1) * HEAD_DIM)
+                    nc.tensor.matmul(
+                        out=turned[:, cols],
+                        lhsT=by_cos[:, h, tokens],
+                        rhs=ident[:],
+                        start=True,
+                        stop=False,
+                        is_transpose=True,
+                    )
+                    nc.tensor.matmul(
+                        out=turned[:, cols],
+                        lhsT=by_sin[:, h, tokens],
+                        rhs=swap[:],
+                        start=False,
+                        stop=True,
+                        is_transpose=True,
+                    )
+                nc.scalar.copy(out=rotated[:, t, :], in_=turned[:])
             tiles = slice(c * CHUNK_TILES, (c + 1) * CHUNK_TILES)
             nc.sync.dma_start(out=out_rows[half][:, tiles, :], in_=rotated[:])
 
+        chunk_inputs = prepare_chunk(0)
+        waiting = None
         for c in range(CHUNKS):
-            project_and_rotate(c, 0, operand[0], operand[1])
-            following = quantise_chunk(c + 1) if c + 1 < CHUNKS else None
-            project_and_rotate(c, 1, operand[0], operand[1])
-            operand = following
+            for half in range(2):
+                fresh = multiply(half, *chunk_inputs)
+                if half == 0 and c + 1 < CHUNKS:
+                    next_inputs = prepare_chunk(c + 1)
+                if waiting is not None:
+                    turn_back(*waiting)
+                waiting = (c, half) + fresh
+            chunk_inputs = next_inputs
+        turn_back(*waiting)

@@ -49,7 +49,7 @@ def tile_moonvitvisiontower_pa_t_kernel(
         keep = ctx.enter_context(tc.tile_pool(name="keep", bufs=1))
         stage = ctx.enter_context(tc.tile_pool(name="stage", bufs=2))
         products = ctx.enter_context(tc.tile_pool(name="products", bufs=3))
-        results = ctx.enter_context(tc.tile_pool(name="results", bufs=3))
+        results = ctx.enter_context(tc.tile_pool(name="results", bufs=4))
         psum_prep = ctx.enter_context(tc.psum_pool(name="psum_prep", bufs=2))
         psum_mx = ctx.enter_context(tc.psum_pool(name="psum_mx", bufs=4))
         psum_out = ctx.enter_context(tc.psum_pool(name="psum_out", bufs=2))
@@ -101,67 +101,50 @@ def tile_moonvitvisiontower_pa_t_kernel(
         consts = keep.tile([P, SIGN + 1], F32)
         nc.vector.tensor_copy(out=consts[:], in_=consts_ps[:, 0 : SIGN + 1])
 
-        def prepare_chunk(c):
-            grouped = stage.tile([P, CHUNK_TOKENS * PACK], BF16, align_bytes=64)
+        def transpose_x(c, first, grouped):
             grouped_words = grouped[:].bitcast(F32).rearrange(
                 "p (t m u) -> p t m u", t=CHUNK_TILES, u=2
             )
-            for first in range(0, CHUNK_TILES, 2):
-                x_t = psum_prep.tile([P, 2, 2, P], F32, tag="prep")
-                for i in range(2):
-                    words = x_sb[:, c * CHUNK_TILES + first + i, :].bitcast(F32)
-                    for u in range(2):
-                        nc.tensor.transpose(x_t[:, i, u, :], words[:, u : K // 2 : 2], ident[:])
-                nc.scalar.copy(
-                    out=grouped_words[:, first : first + 2, :, :],
-                    in_=x_t[:].rearrange("p i u m -> p i m u"),
-                )
-
-            tiles = slice(c * CHUNK_TILES, (c + 1) * CHUNK_TILES)
-            wide = [P, CHUNK_TILES, PAIRS, 2]
-            cos_wide = stage.tile(wide, F32)
-            sin_wide = stage.tile(wide, F32)
-            for doubled, single in ((cos_wide, cos_sb), (sin_wide, sin_sb)):
-                nc.gpsimd.tensor_scalar(
-                    out=doubled[:],
-                    in0=single[:, tiles, :].unsqueeze(3).to_broadcast(wide),
-                    scalar1=1.0,
-                    scalar2=0.0,
-                    op0=MULT,
-                    op1=ADD,
-                )
-            cos_ps = psum_prep.tile([P, CHUNK_TOKENS], F32, tag="prep")
-            for t in range(CHUNK_TILES):
-                nc.tensor.transpose(
-                    cos_ps[:, t * P : (t + 1) * P],
-                    cos_wide[:, t].rearrange("p j e -> p (j e)"),
-                    ident[:],
-                )
-            cos_t = stage.tile([P, CHUNK_TOKENS], F32)
-            nc.scalar.copy(out=cos_t[:], in_=cos_ps[:])
-            sin_ps = psum_prep.tile([P, CHUNK_TOKENS], F32, tag="prep")
-            for t in range(CHUNK_TILES):
-                nc.tensor.transpose(
-                    sin_ps[:, t * P : (t + 1) * P],
-                    sin_wide[:, t].rearrange("p j e -> p (j e)"),
-                    ident[:],
-                )
-            sin_t = stage.tile([P, CHUNK_TOKENS], F32)
-            nc.scalar.activation(
-                out=sin_t[:], in_=sin_ps[:], func=COPY, scale=consts[:, SIGN : SIGN + 1]
+            x_t = psum_prep.tile([P, 2, 2, P], F32, tag="prep")
+            for i in range(2):
+                words = x_sb[:, c * CHUNK_TILES + first + i, :].bitcast(F32)
+                for u in range(2):
+                    nc.tensor.transpose(x_t[:, i, u, :], words[:, u : K // 2 : 2], ident[:])
+            nc.scalar.copy(
+                out=grouped_words[:, first : first + 2, :, :],
+                in_=x_t[:].rearrange("p i u m -> p i m u"),
             )
 
+        def quantise(grouped):
             x_codes = stage.tile([P, CHUNK_TOKENS], U32, align_bytes=64)
             x_scales = stage.tile([P, CHUNK_TOKENS], U8, align_bytes=64)
             nc.vector.quantize_mx(
                 out=x_codes[:].bitcast(FP8X4), scales=x_scales[:], in_=grouped[:]
             )
-            return x_codes, x_scales, cos_t, sin_t
+            return x_codes, x_scales
 
-        def multiply(half, x_codes, x_scales, cos_t, sin_t):
-            by_cos = products.tile([P, HEADS, CHUNK_TOKENS], F32)
-            by_sin = products.tile([P, HEADS, CHUNK_TOKENS], F32)
-            for h in range(HEADS):
+        def transpose_table(c, rows, table, scale):
+            tiles = slice(c * CHUNK_TILES, (c + 1) * CHUNK_TILES)
+            doubled = stage.tile([P, CHUNK_TILES, PAIRS, 2], F32)
+            nc.gpsimd.tensor_scalar(
+                out=doubled[:],
+                in0=rows[:, tiles, :].unsqueeze(3).to_broadcast([P, CHUNK_TILES, PAIRS, 2]),
+                scalar1=1.0,
+                scalar2=0.0,
+                op0=MULT,
+                op1=ADD,
+            )
+            table_ps = psum_prep.tile([P, CHUNK_TOKENS], F32, tag="prep")
+            for t in range(CHUNK_TILES):
+                nc.tensor.transpose(
+                    table_ps[:, t * P : (t + 1) * P],
+                    doubled[:, t].rearrange("p j e -> p (j e)"),
+                    ident[:],
+                )
+            nc.scalar.activation(out=table[:], in_=table_ps[:], func=COPY, scale=scale)
+
+        def multiply(by_cos, by_sin, half, first, x_codes, x_scales, cos_t, sin_t):
+            for h in range(first, first + 2):
                 head = half * HEADS + h
                 cols = slice(head * HEAD_DIM, (head + 1) * HEAD_DIM)
                 col_bytes = slice(2 * head * HEAD_DIM, 2 * (head + 1) * HEAD_DIM)
@@ -184,12 +167,11 @@ def tile_moonvitvisiontower_pa_t_kernel(
                         op0=ADD,
                         op1=MULT,
                     )
-            return by_cos, by_sin
 
-        def turn_back(c, half, by_cos, by_sin):
-            rotated = results.tile([P, CHUNK_TILES, HALF], F32)
-            for t in range(CHUNK_TILES):
-                tokens = slice(t * P, (t + 1) * P)
+        def turn_back(c, half, first, by_cos, by_sin):
+            rotated = results.tile([P, 2, HALF], F32)
+            for i in range(2):
+                tokens = slice((first + i) * P, (first + i + 1) * P)
                 turned = psum_out.tile([P, HALF], F32)
                 for h in range(HEADS):
                     cols = slice(h * HEAD_DIM, (h + 1) * HEAD_DIM)
@@ -209,19 +191,62 @@ def tile_moonvitvisiontower_pa_t_kernel(
                         stop=True,
                         is_transpose=True,
                     )
-                nc.scalar.copy(out=rotated[:, t, :], in_=turned[:])
-            tiles = slice(c * CHUNK_TILES, (c + 1) * CHUNK_TILES)
+                nc.scalar.copy(out=rotated[:, i, :], in_=turned[:])
+            tiles = slice(c * CHUNK_TILES + first, c * CHUNK_TILES + first + 2)
             nc.sync.dma_start(out=out_rows[half][:, tiles, :], in_=rotated[:])
 
-        chunk_inputs = prepare_chunk(0)
-        waiting = None
+        def new_chunk_tiles():
+            grouped = stage.tile([P, CHUNK_TOKENS * PACK], BF16, align_bytes=64)
+            cos_t = stage.tile([P, CHUNK_TOKENS], F32)
+            sin_t = stage.tile([P, CHUNK_TOKENS], F32)
+            return grouped, cos_t, sin_t
+
+        def new_products():
+            by_cos = products.tile([P, HEADS, CHUNK_TOKENS], F32)
+            by_sin = products.tile([P, HEADS, CHUNK_TOKENS], F32)
+            return by_cos, by_sin
+
+        sign = consts[:, SIGN : SIGN + 1]
+
+        grouped, cos_t, sin_t = new_chunk_tiles()
+        transpose_x(0, 0, grouped)
+        transpose_x(0, 2, grouped)
+        transpose_table(0, cos_sb, cos_t, 1.0)
+        transpose_table(0, sin_sb, sin_t, sign)
+        x_codes, x_scales = quantise(grouped)
+
+        keys = None
         for c in range(CHUNKS):
-            for half in range(2):
-                fresh = multiply(half, *chunk_inputs)
-                if half == 0 and c + 1 < CHUNKS:
-                    next_inputs = prepare_chunk(c + 1)
-                if waiting is not None:
-                    turn_back(*waiting)
-                waiting = (c, half) + fresh
-            chunk_inputs = next_inputs
-        turn_back(*waiting)
+            more = c + 1 < CHUNKS
+            inputs = (x_codes, x_scales, cos_t, sin_t)
+            queries = new_products()
+            if more:
+                grouped, next_cos_t, next_sin_t = new_chunk_tiles()
+
+            multiply(*queries, 0, 0, *inputs)
+            if more:
+                transpose_x(c + 1, 0, grouped)
+            if keys is not None:
+                turn_back(c - 1, 1, 0, *keys)
+
+            multiply(*queries, 0, 2, *inputs)
+            if more:
+                transpose_x(c + 1, 2, grouped)
+            if keys is not None:
+                turn_back(c - 1, 1, 2, *keys)
+
+            keys = new_products()
+            multiply(*keys, 1, 0, *inputs)
+            if more:
+                transpose_table(c + 1, cos_sb, next_cos_t, 1.0)
+                x_codes, x_scales = quantise(grouped)
+            turn_back(c, 0, 0, *queries)
+
+            multiply(*keys, 1, 2, *inputs)
+            if more:
+                transpose_table(c + 1, sin_sb, next_sin_t, sign)
+                cos_t, sin_t = next_cos_t, next_sin_t
+            turn_back(c, 0, 2, *queries)
+
+        turn_back(CHUNKS - 1, 1, 0, *keys)
+        turn_back(CHUNKS - 1, 1, 2, *keys)

@@ -31,6 +31,11 @@ SIGN = 2 * HEADS
 
 FLOPS = 2 * TOKENS * K * 2 * HALF
 
+F_CHUNKS = (0, 4)
+A_CHUNKS = (1, 2, 3, 5, 6, 7)
+F_TILES = len(F_CHUNKS) * CHUNK_TILES
+F_PERIOD = 3
+
 
 def tile_moonvitvisiontower_pa_t_kernel(
     tc, x, w_qk_words, w_qk_scales, b_qk, freqs_cos, freqs_sin, out_0, out_1
@@ -50,6 +55,7 @@ def tile_moonvitvisiontower_pa_t_kernel(
         stage = ctx.enter_context(tc.tile_pool(name="stage", bufs=2))
         products = ctx.enter_context(tc.tile_pool(name="products", bufs=3))
         results = ctx.enter_context(tc.tile_pool(name="results", bufs=4))
+        token_major = ctx.enter_context(tc.tile_pool(name="token_major", bufs=2))
         psum_prep = ctx.enter_context(tc.psum_pool(name="psum_prep", bufs=2))
         psum_mx = ctx.enter_context(tc.psum_pool(name="psum_mx", bufs=4))
         psum_out = ctx.enter_context(tc.psum_pool(name="psum_out", bufs=2))
@@ -57,11 +63,13 @@ def tile_moonvitvisiontower_pa_t_kernel(
         x_sb = keep.tile([P, TOKEN_TILES, K], BF16)
         cos_sb = keep.tile([P, TOKEN_TILES, PAIRS], BF16)
         sin_sb = keep.tile([P, TOKEN_TILES, PAIRS], BF16)
+        minus_sin = keep.tile([P, F_TILES, PAIRS], BF16)
         w_words = keep.tile([P, 2 * 2 * HALF], U8, align_bytes=64)
         w_scales = keep.tile([P, 2 * HALF], U8, align_bytes=64)
         const_rows = keep.tile([P, P], BF16)
         ident = keep.tile([P, P], F32)
         swap = keep.tile([P, P], F32)
+        bias_all = keep.tile([P, 2 * HALF], F32)
 
         nc.vector.memset(w_scales[:].bitcast(I32), 0)
         nc.vector.memset(const_rows[:, 0:P:2], 1.0)
@@ -101,7 +109,20 @@ def tile_moonvitvisiontower_pa_t_kernel(
         consts = keep.tile([P, SIGN + 1], F32)
         nc.vector.tensor_copy(out=consts[:], in_=consts_ps[:, 0 : SIGN + 1])
 
-        def transpose_x(c, first, grouped):
+        for half in range(2):
+            bias_ps = psum_prep.tile([P, HALF], F32, tag="prep")
+            for h in range(HEADS):
+                head = half * HEADS + h
+                nc.tensor.transpose(
+                    bias_ps[:, h * HEAD_DIM : (h + 1) * HEAD_DIM],
+                    consts[:, head : head + 1].to_broadcast([P, P]),
+                    ident[:],
+                )
+            nc.vector.tensor_copy(
+                out=bias_all[:, half * HALF : (half + 1) * HALF], in_=bias_ps[:]
+            )
+
+        def transpose_x(c, first, grouped, copy):
             grouped_words = grouped[:].bitcast(F32).rearrange(
                 "p (t m u) -> p t m u", t=CHUNK_TILES, u=2
             )
@@ -110,30 +131,26 @@ def tile_moonvitvisiontower_pa_t_kernel(
                 words = x_sb[:, c * CHUNK_TILES + first + i, :].bitcast(F32)
                 for u in range(2):
                     nc.tensor.transpose(x_t[:, i, u, :], words[:, u : K // 2 : 2], ident[:])
-            nc.scalar.copy(
+            copy(
                 out=grouped_words[:, first : first + 2, :, :],
                 in_=x_t[:].rearrange("p i u m -> p i m u"),
             )
 
-        def quantise(grouped):
-            x_codes = stage.tile([P, CHUNK_TOKENS], U32, align_bytes=64)
-            x_scales = stage.tile([P, CHUNK_TOKENS], U8, align_bytes=64)
+        def quantise(grouped, x_codes, x_scales):
             nc.vector.quantize_mx(
                 out=x_codes[:].bitcast(FP8X4), scales=x_scales[:], in_=grouped[:]
             )
-            return x_codes, x_scales
 
-        def transpose_table(c, rows, table, scale):
+        def double_table(c, rows):
             tiles = slice(c * CHUNK_TILES, (c + 1) * CHUNK_TILES)
             doubled = stage.tile([P, CHUNK_TILES, PAIRS, 2], F32)
-            nc.gpsimd.tensor_scalar(
+            nc.scalar.copy(
                 out=doubled[:],
-                in0=rows[:, tiles, :].unsqueeze(3).to_broadcast([P, CHUNK_TILES, PAIRS, 2]),
-                scalar1=1.0,
-                scalar2=0.0,
-                op0=MULT,
-                op1=ADD,
+                in_=rows[:, tiles, :].unsqueeze(3).to_broadcast([P, CHUNK_TILES, PAIRS, 2]),
             )
+            return doubled
+
+        def transpose_table(doubled, table, scale):
             table_ps = psum_prep.tile([P, CHUNK_TOKENS], F32, tag="prep")
             for t in range(CHUNK_TILES):
                 nc.tensor.transpose(
@@ -195,11 +212,106 @@ def tile_moonvitvisiontower_pa_t_kernel(
             tiles = slice(c * CHUNK_TILES + first, c * CHUNK_TILES + first + 2)
             nc.sync.dma_start(out=out_rows[half][:, tiles, :], in_=rotated[:])
 
+        f_operands = []
+        for n in range(len(F_CHUNKS)):
+            f_codes = keep.tile([P, CHUNK_TOKENS], U32, align_bytes=64, name="f_codes%d" % n)
+            f_scales = keep.tile([P, CHUNK_TOKENS], U8, align_bytes=64, name="f_scales%d" % n)
+            f_operands.append((f_codes, f_scales))
+
+        def negate_sin(n):
+            tiles = slice(F_CHUNKS[n] * CHUNK_TILES, (F_CHUNKS[n] + 1) * CHUNK_TILES)
+            nc.scalar.activation(
+                out=minus_sin[:, n * CHUNK_TILES : (n + 1) * CHUNK_TILES, :],
+                in_=sin_sb[:, tiles, :],
+                func=COPY,
+                scale=-1.0,
+            )
+
+        def f_pass(i, half, biased):
+            f_codes, f_scales = f_operands[i // CHUNK_TILES]
+            tokens = slice((i % CHUNK_TILES) * P, (i % CHUNK_TILES + 1) * P)
+            acc = psum_prep.tile([P, HALF], F32, tag="prep")
+            nc.tensor.matmul_mx(
+                out=acc[:],
+                lhsT=f_codes[:, tokens].bitcast(FP8X4),
+                lhsT_scale=f_scales[:, tokens],
+                rhs=w_words[:, 2 * half * HALF : 2 * (half + 1) * HALF].bitcast(FP4X4),
+                rhs_scale=w_scales[:, half * HALF : (half + 1) * HALF],
+                start=True,
+                stop=True,
+            )
+            nc.vector.tensor_tensor(
+                out=biased[:, half * HEADS : (half + 1) * HEADS, :, :],
+                in0=acc[:].rearrange("p (h j e) -> p h e j", h=HEADS, e=2),
+                in1=bias_all[:, half * HALF : (half + 1) * HALF].rearrange(
+                    "p (h j e) -> p h e j", h=HEADS, e=2
+                ),
+                op=ADD,
+            )
+
+        def f_rotate(i, biased):
+            g = F_CHUNKS[i // CHUNK_TILES] * CHUNK_TILES + i % CHUNK_TILES
+            by_c = token_major.tile([P, 2 * HEADS, 2, PAIRS], F32)
+            by_s = token_major.tile([P, 2 * HEADS, 2, PAIRS], F32)
+            rot = token_major.tile([P, 2 * HEADS, PAIRS, 2], F32)
+            nc.gpsimd.tensor_tensor(
+                out=by_c[:].rearrange("p a e j -> p (a e) j"),
+                in0=biased[:].rearrange("p a e j -> p (a e) j"),
+                in1=cos_sb[:, g, :].unsqueeze(1).to_broadcast([P, 4 * HEADS, PAIRS]),
+                op=MULT,
+            )
+            nc.gpsimd.tensor_tensor(
+                out=by_s[:, :, 0, :],
+                in0=biased[:, :, 1, :],
+                in1=minus_sin[:, i, :].unsqueeze(1).to_broadcast([P, 2 * HEADS, PAIRS]),
+                op=MULT,
+            )
+            nc.gpsimd.tensor_tensor(
+                out=by_s[:, :, 1, :],
+                in0=biased[:, :, 0, :],
+                in1=sin_sb[:, g, :].unsqueeze(1).to_broadcast([P, 2 * HEADS, PAIRS]),
+                op=MULT,
+            )
+            nc.gpsimd.tensor_tensor(
+                out=rot[:],
+                in0=by_c[:].rearrange("p a e j -> p a j e"),
+                in1=by_s[:].rearrange("p a e j -> p a j e"),
+                op=ADD,
+            )
+            return rot
+
+        def f_store(i, rot):
+            g = F_CHUNKS[i // CHUNK_TILES] * CHUNK_TILES + i % CHUNK_TILES
+            for half in range(2):
+                nc.sync.dma_start(
+                    out=out_rows[half][:, g, :],
+                    in_=rot[:, half * HEADS : (half + 1) * HEADS, :, :].rearrange(
+                        "p h j e -> p (h j e)"
+                    ),
+                )
+
+        f_state = {}
+
+        def f_step(count):
+            i = count // F_PERIOD
+            phase = count % F_PERIOD
+            if i < F_TILES and phase == 0:
+                biased = token_major.tile([P, 2 * HEADS, 2, PAIRS], F32)
+                f_state["biased"] = biased
+                f_pass(i, 0, biased)
+            if i < F_TILES and phase == 1:
+                f_pass(i, 1, f_state["biased"])
+                f_state[i] = f_rotate(i, f_state["biased"])
+            if phase == 1 and 1 <= i <= F_TILES:
+                f_store(i - 1, f_state[i - 1])
+
         def new_chunk_tiles():
             grouped = stage.tile([P, CHUNK_TOKENS * PACK], BF16, align_bytes=64)
             cos_t = stage.tile([P, CHUNK_TOKENS], F32)
             sin_t = stage.tile([P, CHUNK_TOKENS], F32)
-            return grouped, cos_t, sin_t
+            x_codes = stage.tile([P, CHUNK_TOKENS], U32, align_bytes=64)
+            x_scales = stage.tile([P, CHUNK_TOKENS], U8, align_bytes=64)
+            return grouped, cos_t, sin_t, x_codes, x_scales
 
         def new_products():
             by_cos = products.tile([P, HEADS, CHUNK_TOKENS], F32)
@@ -208,45 +320,67 @@ def tile_moonvitvisiontower_pa_t_kernel(
 
         sign = consts[:, SIGN : SIGN + 1]
 
-        grouped, cos_t, sin_t = new_chunk_tiles()
-        transpose_x(0, 0, grouped)
-        transpose_x(0, 2, grouped)
-        transpose_table(0, cos_sb, cos_t, 1.0)
-        transpose_table(0, sin_sb, sin_t, sign)
-        x_codes, x_scales = quantise(grouped)
+        grouped_f = stage.tile([P, CHUNK_TOKENS * PACK], BF16, align_bytes=64)
+        grouped, cos_t, sin_t, x_codes, x_scales = new_chunk_tiles()
+        transpose_x(F_CHUNKS[0], 0, grouped_f, nc.vector.tensor_copy)
+        transpose_x(F_CHUNKS[0], 2, grouped_f, nc.vector.tensor_copy)
+        negate_sin(0)
+        transpose_x(A_CHUNKS[0], 0, grouped, nc.scalar.copy)
+        transpose_x(A_CHUNKS[0], 2, grouped, nc.scalar.copy)
+        quantise(grouped_f, *f_operands[0])
+        doubled_cos = double_table(A_CHUNKS[0], cos_sb)
+        doubled_sin = double_table(A_CHUNKS[0], sin_sb)
+        f_step(0)
+        f_step(1)
+        transpose_table(doubled_cos, cos_t, 1.0)
+        transpose_table(doubled_sin, sin_t, sign)
+        quantise(grouped, x_codes, x_scales)
 
-        keys = None
-        for c in range(CHUNKS):
-            more = c + 1 < CHUNKS
+        before = None
+        for a in range(len(A_CHUNKS)):
+            c = A_CHUNKS[a]
+            more = a + 1 < len(A_CHUNKS)
+            following = A_CHUNKS[a + 1] if more else None
             inputs = (x_codes, x_scales, cos_t, sin_t)
-            queries = new_products()
             if more:
-                grouped, next_cos_t, next_sin_t = new_chunk_tiles()
-
-            multiply(*queries, 0, 0, *inputs)
+                grouped, next_cos_t, next_sin_t, next_codes, next_scales = new_chunk_tiles()
+            queries = None
+            keys = None
+            for q in range(4):
+                step = 4 * a + q
+                f_step(step + F_PERIOD)
+                if q == 0:
+                    queries = new_products()
+                if q == 2:
+                    keys = new_products()
+                unit = queries if q < 2 else keys
+                multiply(*unit, q // 2, 2 * (q % 2), *inputs)
+                if more and q < 2:
+                    transpose_x(following, 2 * q, grouped, nc.scalar.copy)
+                if more and q == 2:
+                    transpose_table(doubled_cos, next_cos_t, 1.0)
+                    quantise(grouped, next_codes, next_scales)
+                if more and q == 3:
+                    transpose_table(doubled_sin, next_sin_t, sign)
+                if step == 2:
+                    grouped_f = stage.tile([P, CHUNK_TOKENS * PACK], BF16, align_bytes=64)
+                    transpose_x(F_CHUNKS[1], 0, grouped_f, nc.scalar.copy)
+                if step == 5:
+                    transpose_x(F_CHUNKS[1], 2, grouped_f, nc.scalar.copy)
+                    negate_sin(1)
+                if step == 6:
+                    quantise(grouped_f, *f_operands[1])
+                if q < 2 and before is not None:
+                    turn_back(before[0], 1, 2 * q, *before[1])
+                if q >= 2:
+                    turn_back(c, 0, 2 * (q - 2), *queries)
+                if more and q == 0:
+                    doubled_cos = double_table(following, cos_sb)
+                if more and q == 1:
+                    doubled_sin = double_table(following, sin_sb)
+            before = (c, keys)
             if more:
-                transpose_x(c + 1, 0, grouped)
-            if keys is not None:
-                turn_back(c - 1, 1, 0, *keys)
+                x_codes, x_scales, cos_t, sin_t = next_codes, next_scales, next_cos_t, next_sin_t
 
-            multiply(*queries, 0, 2, *inputs)
-            if more:
-                transpose_x(c + 1, 2, grouped)
-            if keys is not None:
-                turn_back(c - 1, 1, 2, *keys)
-
-            keys = new_products()
-            multiply(*keys, 1, 0, *inputs)
-            if more:
-                transpose_table(c + 1, cos_sb, next_cos_t, 1.0)
-                x_codes, x_scales = quantise(grouped)
-            turn_back(c, 0, 0, *queries)
-
-            multiply(*keys, 1, 2, *inputs)
-            if more:
-                transpose_table(c + 1, sin_sb, next_sin_t, sign)
-                cos_t, sin_t = next_cos_t, next_sin_t
-            turn_back(c, 0, 2, *queries)
-
-        turn_back(CHUNKS - 1, 1, 0, *keys)
-        turn_back(CHUNKS - 1, 1, 2, *keys)
+        turn_back(before[0], 1, 0, *before[1])
+        turn_back(before[0], 1, 2, *before[1])

@@ -63,7 +63,8 @@ def tile_moonvitvisiontower_pa_t_kernel(
         x_sb = keep.tile([P, TOKEN_TILES, K], BF16)
         cos_sb = keep.tile([P, TOKEN_TILES, PAIRS], BF16)
         sin_sb = keep.tile([P, TOKEN_TILES, PAIRS], BF16)
-        minus_sin = keep.tile([P, F_TILES, PAIRS], BF16)
+        f_cos = keep.tile([P, F_TILES, PAIRS, 2], BF16)
+        f_sin = keep.tile([P, F_TILES, PAIRS, 2], BF16)
         w_words = keep.tile([P, 2 * 2 * HALF], U8, align_bytes=64)
         w_scales = keep.tile([P, 2 * HALF], U8, align_bytes=64)
         const_rows = keep.tile([P, P], BF16)
@@ -220,12 +221,15 @@ def tile_moonvitvisiontower_pa_t_kernel(
 
         def negate_sin(n):
             tiles = slice(F_CHUNKS[n] * CHUNK_TILES, (F_CHUNKS[n] + 1) * CHUNK_TILES)
-            nc.scalar.activation(
-                out=minus_sin[:, n * CHUNK_TILES : (n + 1) * CHUNK_TILES, :],
-                in_=sin_sb[:, tiles, :],
-                func=COPY,
-                scale=-1.0,
+            items = slice(n * CHUNK_TILES, (n + 1) * CHUNK_TILES)
+            nc.scalar.copy(
+                out=f_cos[:, items, :, :],
+                in_=cos_sb[:, tiles, :].unsqueeze(3).to_broadcast([P, CHUNK_TILES, PAIRS, 2]),
             )
+            nc.scalar.activation(
+                out=f_sin[:, items, :, 0], in_=sin_sb[:, tiles, :], func=COPY, scale=-1.0
+            )
+            nc.scalar.copy(out=f_sin[:, items, :, 1], in_=sin_sb[:, tiles, :])
 
         def f_pass(i, half, biased):
             f_codes, f_scales = f_operands[i // CHUNK_TILES]
@@ -241,41 +245,36 @@ def tile_moonvitvisiontower_pa_t_kernel(
                 stop=True,
             )
             nc.vector.tensor_tensor(
-                out=biased[:, half * HEADS : (half + 1) * HEADS, :, :],
-                in0=acc[:].rearrange("p (h j e) -> p h e j", h=HEADS, e=2),
-                in1=bias_all[:, half * HALF : (half + 1) * HALF].rearrange(
-                    "p (h j e) -> p h e j", h=HEADS, e=2
+                out=biased[:, half * HEADS : (half + 1) * HEADS, :, :].rearrange(
+                    "p h j e -> p (h j e)"
                 ),
+                in0=acc[:],
+                in1=bias_all[:, half * HALF : (half + 1) * HALF],
                 op=ADD,
             )
 
         def f_rotate(i, biased):
             g = F_CHUNKS[i // CHUNK_TILES] * CHUNK_TILES + i % CHUNK_TILES
-            by_c = token_major.tile([P, 2 * HEADS, 2, PAIRS], F32)
-            by_s = token_major.tile([P, 2 * HEADS, 2, PAIRS], F32)
+            by_c = token_major.tile([P, 2 * HEADS, PAIRS, 2], F32)
+            by_s = token_major.tile([P, 2 * HEADS, PAIRS, 2], F32)
             rot = token_major.tile([P, 2 * HEADS, PAIRS, 2], F32)
+            whole = [P, 2 * HEADS, PAIRS, 2]
             nc.gpsimd.tensor_tensor(
-                out=by_c[:].rearrange("p a e j -> p (a e) j"),
-                in0=biased[:].rearrange("p a e j -> p (a e) j"),
-                in1=cos_sb[:, g, :].unsqueeze(1).to_broadcast([P, 4 * HEADS, PAIRS]),
+                out=by_c[:],
+                in0=biased[:],
+                in1=f_cos[:, i, :, :].unsqueeze(1).to_broadcast(whole),
                 op=MULT,
             )
             nc.gpsimd.tensor_tensor(
-                out=by_s[:, :, 0, :],
-                in0=biased[:, :, 1, :],
-                in1=minus_sin[:, i, :].unsqueeze(1).to_broadcast([P, 2 * HEADS, PAIRS]),
+                out=by_s[:],
+                in0=biased[:, :, :, ::-1],
+                in1=f_sin[:, i, :, :].unsqueeze(1).to_broadcast(whole),
                 op=MULT,
             )
             nc.gpsimd.tensor_tensor(
-                out=by_s[:, :, 1, :],
-                in0=biased[:, :, 0, :],
-                in1=sin_sb[:, g, :].unsqueeze(1).to_broadcast([P, 2 * HEADS, PAIRS]),
-                op=MULT,
-            )
-            nc.gpsimd.tensor_tensor(
-                out=rot[:],
-                in0=by_c[:].rearrange("p a e j -> p a j e"),
-                in1=by_s[:].rearrange("p a e j -> p a j e"),
+                out=rot[:].rearrange("p a j e -> p (a j e)"),
+                in0=by_c[:].rearrange("p a j e -> p (a j e)"),
+                in1=by_s[:].rearrange("p a j e -> p (a j e)"),
                 op=ADD,
             )
             return rot
@@ -296,7 +295,7 @@ def tile_moonvitvisiontower_pa_t_kernel(
             i = count // F_PERIOD
             phase = count % F_PERIOD
             if i < F_TILES and phase == 0:
-                biased = token_major.tile([P, 2 * HEADS, 2, PAIRS], F32)
+                biased = token_major.tile([P, 2 * HEADS, PAIRS, 2], F32)
                 f_state["biased"] = biased
                 f_pass(i, 0, biased)
             if i < F_TILES and phase == 1:

@@ -54,8 +54,8 @@ def tile_moonvitvisiontower_pa_t_kernel(
         keep = ctx.enter_context(tc.tile_pool(name="keep", bufs=1))
         stage = ctx.enter_context(tc.tile_pool(name="stage", bufs=2))
         products = ctx.enter_context(tc.tile_pool(name="products", bufs=3))
-        results = ctx.enter_context(tc.tile_pool(name="results", bufs=4))
-        token_major = ctx.enter_context(tc.tile_pool(name="token_major", bufs=2))
+        results = ctx.enter_context(tc.tile_pool(name="results", bufs=8))
+        token_major = ctx.enter_context(tc.tile_pool(name="token_major", bufs=3))
         psum_prep = ctx.enter_context(tc.psum_pool(name="psum_prep", bufs=2))
         psum_mx = ctx.enter_context(tc.psum_pool(name="psum_mx", bufs=4))
         psum_out = ctx.enter_context(tc.psum_pool(name="psum_out", bufs=2))
@@ -190,7 +190,7 @@ def tile_moonvitvisiontower_pa_t_kernel(
             rotated = results.tile([P, 2, HALF], F32)
             for i in range(2):
                 tokens = slice((first + i) * P, (first + i + 1) * P)
-                turned = psum_out.tile([P, HALF], F32)
+                turned = psum_out.tile([P, HALF], F32, tag="turned")
                 for h in range(HEADS):
                     cols = slice(h * HEAD_DIM, (h + 1) * HEAD_DIM)
                     nc.tensor.matmul(
@@ -212,6 +212,30 @@ def tile_moonvitvisiontower_pa_t_kernel(
                 nc.scalar.copy(out=rotated[:, i, :], in_=turned[:])
             tiles = slice(c * CHUNK_TILES + first, c * CHUNK_TILES + first + 2)
             nc.sync.dma_start(out=out_rows[half][:, tiles, :], in_=rotated[:])
+
+        def turn_back_by_heads(c, half, by_cos, by_sin):
+            first_two = [psum_prep.tile([P, HALF], F32, tag="prep", name="open%d" % t) for t in range(2)]
+            last_two = [psum_out.tile([P, HALF], F32, tag="turned", name="open%d" % t) for t in (2, 3)]
+            open_banks = first_two + last_two
+            order = [(h, t) for t in (0, 1) for h in (0, 1)] + [(h, t) for t in (2, 3) for h in (0, 1)]
+            order += [(h, t) for h in (2, 3) for t in range(CHUNK_TILES)]
+            for h, t in order:
+                cols = slice(h * HEAD_DIM, (h + 1) * HEAD_DIM)
+                tokens = slice(t * P, (t + 1) * P)
+                nc.tensor.matmul(
+                    out=open_banks[t][:, cols], lhsT=by_cos[:, h, tokens], rhs=ident[:],
+                    start=True, stop=False, is_transpose=True,
+                )
+                nc.tensor.matmul(
+                    out=open_banks[t][:, cols], lhsT=by_sin[:, h, tokens], rhs=swap[:],
+                    start=False, stop=True, is_transpose=True,
+                )
+            for first in (0, 2):
+                rotated = results.tile([P, 2, HALF], F32)
+                nc.scalar.copy(out=rotated[:, 0, :], in_=open_banks[first][:])
+                nc.vector.tensor_copy(out=rotated[:, 1, :], in_=open_banks[first + 1][:])
+                tiles = slice(c * CHUNK_TILES + first, c * CHUNK_TILES + first + 2)
+                nc.sync.dma_start(out=out_rows[half][:, tiles, :], in_=rotated[:])
 
         f_operands = []
         for n in range(len(F_CHUNKS)):
@@ -381,5 +405,4 @@ def tile_moonvitvisiontower_pa_t_kernel(
             if more:
                 x_codes, x_scales, cos_t, sin_t = next_codes, next_scales, next_cos_t, next_sin_t
 
-        turn_back(before[0], 1, 0, *before[1])
-        turn_back(before[0], 1, 2, *before[1])
+        turn_back_by_heads(before[0], 1, *before[1])

from contextlib import ExitStack

import concourse.masks as masks
import concourse.mybir as mybir

F32 = mybir.dt.float32
BF16 = mybir.dt.bfloat16
U8 = mybir.dt.uint8
U32 = mybir.dt.uint32
I32 = mybir.dt.int32
FP8X4 = mybir.dt.float8_e4m3fn_x4
FP4X4 = mybir.dt.float4_e2m1fn_x4
MULT = mybir.AluOpType.mult
ADD = mybir.AluOpType.add
COPY = mybir.ActivationFunctionType.Copy

P = 128
PACK = 4
TOKENS = 4096
K = P * PACK
HEADS = 4
HEAD_DIM = 128
PAIRS = HEAD_DIM // 2
HALF = HEADS * HEAD_DIM
TOKEN_TILES = TOKENS // P
CHUNK_TILES = 4
CHUNK_TOKENS = CHUNK_TILES * P
CHUNKS = TOKEN_TILES // CHUNK_TILES
SCALE_ROWS = 4
SIGN = 2 * HEADS

FLOPS = 2 * TOKENS * K * 2 * HALF

F_CHUNKS = (0, 4)
A_CHUNKS = (1, 2, 3, 5, 6, 7)
F_TILES = len(F_CHUNKS) * CHUNK_TILES
F_PERIOD = 3


def tile_moonvitvisiontower_pa_t_kernel(
    tc, x, w_qk_words, w_qk_scales, b_qk, freqs_cos, freqs_sin, out_0, out_1
):
    nc = tc.nc
    x_rows = x.rearrange("(p g) k -> p g k", g=TOKEN_TILES)
    cos_rows = freqs_cos.rearrange("(p g) j -> p g j", g=TOKEN_TILES)
    sin_rows = freqs_sin.rearrange("(p g) j -> p g j", g=TOKEN_TILES)
    out_rows = [
        out_0.rearrange("(p g) h d -> p g (h d)", g=TOKEN_TILES),
        out_1.rearrange("(p g) h d -> p g (h d)", g=TOKEN_TILES),
    ]

    with ExitStack() as ctx:
        ctx.enter_context(tc.manual_schedule())
        keep = ctx.enter_context(tc.tile_pool(name="keep", bufs=1))
        stage = ctx.enter_context(tc.tile_pool(name="stage", bufs=2))
        products = ctx.enter_context(tc.tile_pool(name="products", bufs=3))
        results = ctx.enter_context(tc.tile_pool(name="results", bufs=8))
        token_major = ctx.enter_context(tc.tile_pool(name="token_major", bufs=3))
        psum_prep = ctx.enter_context(tc.psum_pool(name="psum_prep", bufs=2))
        psum_mx = ctx.enter_context(tc.psum_pool(name="psum_mx", bufs=4))
        psum_out = ctx.enter_context(tc.psum_pool(name="psum_out", bufs=2))

        x_sb = keep.tile([P, TOKEN_TILES, K], BF16)
        cos_sb = keep.tile([P, TOKEN_TILES, PAIRS], BF16)
        sin_sb = keep.tile([P, TOKEN_TILES, PAIRS], BF16)
        f_cos = keep.tile([P, F_TILES, PAIRS, 2], BF16)
        f_sin = keep.tile([P, F_TILES, PAIRS, 2], BF16)
        w_words = keep.tile([P, 2 * 2 * HALF], U8, align_bytes=64)
        w_scales = keep.tile([P, 2 * HALF], U8, align_bytes=64)
        const_rows = keep.tile([P, P], BF16)
        ident = keep.tile([P, P], F32)
        swap = keep.tile([P, P], F32)
        bias_all = keep.tile([P, 2 * HALF], F32)

        nc.vector.memset(w_scales[:].bitcast(I32), 0)
        nc.vector.memset(const_rows[:, 0:P:2], 1.0)
        nc.vector.memset(const_rows[:, 1:P:2], -1.0)
        masks.make_identity(nc, ident[:])

        def load_chunk(c):
            tiles = slice(c * CHUNK_TILES, (c + 1) * CHUNK_TILES)
            nc.sync.dma_start(out=x_sb[:, tiles, :], in_=x_rows[:, tiles, :])
            nc.sync.dma_start(out=cos_sb[:, tiles, :], in_=cos_rows[:, tiles, :])
            nc.sync.dma_start(out=sin_sb[:, tiles, :], in_=sin_rows[:, tiles, :])

        nc.sync.dma_start(
            out=const_rows[0 : 2 * HEADS, :], in_=b_qk.rearrange("(r n) -> r n", n=HEAD_DIM)
        )
        load_chunk(0)
        nc.sync.dma_start(out=w_words[:].bitcast(I32), in_=w_qk_words[0].bitcast(I32))
        for quadrant in range(P // 32):
            nc.sync.dma_start(
                out=w_scales[32 * quadrant : 32 * quadrant + SCALE_ROWS, :].bitcast(I32),
                in_=w_qk_scales[
                    0, SCALE_ROWS * quadrant : SCALE_ROWS * (quadrant + 1), :
                ].bitcast(I32),
            )
        for c in range(1, CHUNKS):
            load_chunk(c)

        ident_pairs = ident[:].rearrange("p (j e) -> p j e", e=2)
        swap_pairs = swap[:].rearrange("p (j e) -> p j e", e=2)
        nc.vector.tensor_copy(out=swap_pairs[:, :, 0], in_=ident_pairs[:, :, 1])
        nc.vector.tensor_copy(out=swap_pairs[:, :, 1], in_=ident_pairs[:, :, 0])

        const_rows_f32 = keep.tile([P, P], F32)
        nc.vector.tensor_copy(out=const_rows_f32[:], in_=const_rows[:])
        consts_ps = psum_prep.tile([P, P], F32, tag="prep")
        nc.tensor.transpose(consts_ps[:], const_rows_f32[:], ident[:])
        consts = keep.tile([P, SIGN + 1], F32)
        nc.vector.tensor_copy(out=consts[:], in_=consts_ps[:, 0 : SIGN + 1])

        for half in range(2):
            bias_ps = psum_prep.tile([P, HALF], F32, tag="prep")
            for h in range(HEADS):
                head = half * HEADS + h
                nc.tensor.transpose(
                    bias_ps[:, h * HEAD_DIM : (h + 1) * HEAD_DIM],
                    consts[:, head : head + 1].to_broadcast([P, P]),
                    ident[:],
                )
            nc.vector.tensor_copy(
                out=bias_all[:, half * HALF : (half + 1) * HALF], in_=bias_ps[:]
            )

        def transpose_x(c, first, grouped, copy):
            grouped_words = grouped[:].bitcast(F32).rearrange(
                "p (t m u) -> p t m u", t=CHUNK_TILES, u=2
            )
            x_t = psum_prep.tile([P, 2, 2, P], F32, tag="prep")
            for i in range(2):
                words = x_sb[:, c * CHUNK_TILES + first + i, :].bitcast(F32)
                for u in range(2):
                    nc.tensor.transpose(x_t[:, i, u, :], words[:, u : K // 2 : 2], ident[:])
            copy(
                out=grouped_words[:, first : first + 2, :, :],
                in_=x_t[:].rearrange("p i u m -> p i m u"),
            )

        def quantise(grouped, x_codes, x_scales):
            nc.vector.quantize_mx(
                out=x_codes[:].bitcast(FP8X4), scales=x_scales[:], in_=grouped[:]
            )

        def double_table(c, rows):
            tiles = slice(c * CHUNK_TILES, (c + 1) * CHUNK_TILES)
            doubled = stage.tile([P, CHUNK_TILES, PAIRS, 2], F32)
            nc.scalar.copy(
                out=doubled[:],
                in_=rows[:, tiles, :].unsqueeze(3).to_broadcast([P, CHUNK_TILES, PAIRS, 2]),
            )
            return doubled

        def transpose_table(doubled, table, scale):
            table_ps = psum_prep.tile([P, CHUNK_TOKENS], F32, tag="prep")
            for t in range(CHUNK_TILES):
                nc.tensor.transpose(
                    table_ps[:, t * P : (t + 1) * P],
                    doubled[:, t].rearrange("p j e -> p (j e)"),
                    ident[:],
                )
            nc.scalar.activation(out=table[:], in_=table_ps[:], func=COPY, scale=scale)

        def multiply(by_cos, by_sin, half, first, x_codes, x_scales, cos_t, sin_t):
            for h in range(first, first + 2):
                head = half * HEADS + h
                cols = slice(head * HEAD_DIM, (head + 1) * HEAD_DIM)
                col_bytes = slice(2 * head * HEAD_DIM, 2 * (head + 1) * HEAD_DIM)
                product = psum_mx.tile([P, CHUNK_TOKENS], F32)
                nc.tensor.matmul_mx(
                    out=product[:],
                    lhsT=w_words[:, col_bytes].bitcast(FP4X4),
                    lhsT_scale=w_scales[:, cols],
                    rhs=x_codes[:].bitcast(FP8X4),
                    rhs_scale=x_scales[:],
                    start=True,
                    stop=True,
                )
                for scaled, table in ((by_cos, cos_t), (by_sin, sin_t)):
                    nc.vector.scalar_tensor_tensor(
                        out=scaled[:, h, :],
                        in0=product[:],
                        scalar=consts[:, head : head + 1],
                        in1=table[:],
                        op0=ADD,
                        op1=MULT,
                    )

        def turn_back(c, half, first, by_cos, by_sin):
            rotated = results.tile([P, 2, HALF], F32)
            for i in range(2):
                tokens = slice((first + i) * P, (first + i + 1) * P)
                turned = psum_out.tile([P, HALF], F32, tag="turned")
                for h in range(HEADS):
                    cols = slice(h * HEAD_DIM, (h + 1) * HEAD_DIM)
                    nc.tensor.matmul(
                        out=turned[:, cols],
                        lhsT=by_cos[:, h, tokens],
                        rhs=ident[:],
                        start=True,
                        stop=False,
                        is_transpose=True,
                    )
                    nc.tensor.matmul(
                        out=turned[:, cols],
                        lhsT=by_sin[:, h, tokens],
                        rhs=swap[:],
                        start=False,
                        stop=True,
                        is_transpose=True,
                    )
                nc.scalar.copy(out=rotated[:, i, :], in_=turned[:])
            tiles = slice(c * CHUNK_TILES + first, c * CHUNK_TILES + first + 2)
            nc.sync.dma_start(out=out_rows[half][:, tiles, :], in_=rotated[:])

        def turn_back_by_heads(c, half, by_cos, by_sin):
            first_two = [psum_prep.tile([P, HALF], F32, tag="prep", name="open%d" % t) for t in range(2)]
            last_two = [psum_out.tile([P, HALF], F32, tag="turned", name="open%d" % t) for t in (2, 3)]
            open_banks = first_two + last_two
            order = [(h, t) for t in (0, 1) for h in (0, 1)] + [(h, t) for t in (2, 3) for h in (0, 1)]
            order += [(h, t) for h in (2, 3) for t in range(CHUNK_TILES)]
            for h, t in order:
                cols = slice(h * HEAD_DIM, (h + 1) * HEAD_DIM)
                tokens = slice(t * P, (t + 1) * P)
                nc.tensor.matmul(
                    out=open_banks[t][:, cols], lhsT=by_cos[:, h, tokens], rhs=ident[:],
                    start=True, stop=False, is_transpose=True,
                )
                nc.tensor.matmul(
                    out=open_banks[t][:, cols], lhsT=by_sin[:, h, tokens], rhs=swap[:],
                    start=False, stop=True, is_transpose=True,
                )
            for first in (0, 2):
                rotated = results.tile([P, 2, HALF], F32)
                nc.scalar.copy(out=rotated[:, 0, :], in_=open_banks[first][:])
                nc.vector.tensor_copy(out=rotated[:, 1, :], in_=open_banks[first + 1][:])
                tiles = slice(c * CHUNK_TILES + first, c * CHUNK_TILES + first + 2)
                nc.sync.dma_start(out=out_rows[half][:, tiles, :], in_=rotated[:])

        f_operands = []
        for n in range(len(F_CHUNKS)):
            f_codes = keep.tile([P, CHUNK_TOKENS], U32, align_bytes=64, name="f_codes%d" % n)
            f_scales = keep.tile([P, CHUNK_TOKENS], U8, align_bytes=64, name="f_scales%d" % n)
            f_operands.append((f_codes, f_scales))

        def negate_sin(n):
            tiles = slice(F_CHUNKS[n] * CHUNK_TILES, (F_CHUNKS[n] + 1) * CHUNK_TILES)
            items = slice(n * CHUNK_TILES, (n + 1) * CHUNK_TILES)
            nc.scalar.copy(
                out=f_cos[:, items, :, :],
                in_=cos_sb[:, tiles, :].unsqueeze(3).to_broadcast([P, CHUNK_TILES, PAIRS, 2]),
            )
            nc.scalar.activation(
                out=f_sin[:, items, :, 0], in_=sin_sb[:, tiles, :], func=COPY, scale=-1.0
            )
            nc.scalar.copy(out=f_sin[:, items, :, 1], in_=sin_sb[:, tiles, :])

        def f_pass(i, half, biased):
            f_codes, f_scales = f_operands[i // CHUNK_TILES]
            tokens = slice((i % CHUNK_TILES) * P, (i % CHUNK_TILES + 1) * P)
            acc = psum_prep.tile([P, HALF], F32, tag="prep")
            nc.tensor.matmul_mx(
                out=acc[:],
                lhsT=f_codes[:, tokens].bitcast(FP8X4),
                lhsT_scale=f_scales[:, tokens],
                rhs=w_words[:, 2 * half * HALF : 2 * (half + 1) * HALF].bitcast(FP4X4),
                rhs_scale=w_scales[:, half * HALF : (half + 1) * HALF],
                start=True,
                stop=True,
            )
            nc.vector.tensor_tensor(
                out=biased[:, half * HEADS : (half + 1) * HEADS, :, :].rearrange(
                    "p h j e -> p (h j e)"
                ),
                in0=acc[:],
                in1=bias_all[:, half * HALF : (half + 1) * HALF],
                op=ADD,
            )

        def f_rotate(i, biased):
            g = F_CHUNKS[i // CHUNK_TILES] * CHUNK_TILES + i % CHUNK_TILES
            by_c = token_major.tile([P, 2 * HEADS, PAIRS, 2], F32)
            by_s = token_major.tile([P, 2 * HEADS, PAIRS, 2], F32)
            rot = token_major.tile([P, 2 * HEADS, PAIRS, 2], F32)
            whole = [P, 2 * HEADS, PAIRS, 2]
            nc.gpsimd.tensor_tensor(
                out=by_c[:],
                in0=biased[:],
                in1=f_cos[:, i, :, :].unsqueeze(1).to_broadcast(whole),
                op=MULT,
            )
            nc.gpsimd.tensor_tensor(
                out=by_s[:],
                in0=biased[:, :, :, ::-1],
                in1=f_sin[:, i, :, :].unsqueeze(1).to_broadcast(whole),
                op=MULT,
            )
            nc.gpsimd.tensor_tensor(
                out=rot[:].rearrange("p a j e -> p (a j e)"),
                in0=by_c[:].rearrange("p a j e -> p (a j e)"),
                in1=by_s[:].rearrange("p a j e -> p (a j e)"),
                op=ADD,
            )
            return rot

        def f_store(i, rot):
            g = F_CHUNKS[i // CHUNK_TILES] * CHUNK_TILES + i % CHUNK_TILES
            for half in range(2):
                nc.sync.dma_start(
                    out=out_rows[half][:, g, :],
                    in_=rot[:, half * HEADS : (half + 1) * HEADS, :, :].rearrange(
                        "p h j e -> p (h j e)"
                    ),
                )

        f_state = {}

        def f_step(count):
            i = count // F_PERIOD
            phase = count % F_PERIOD
            if i < F_TILES and phase == 0:
                biased = token_major.tile([P, 2 * HEADS, PAIRS, 2], F32)
                f_state["biased"] = biased
                f_pass(i, 0, biased)
            if i < F_TILES and phase == 1:
                f_pass(i, 1, f_state["biased"])
                f_state[i] = f_rotate(i, f_state["biased"])
            if phase == 1 and 1 <= i <= F_TILES:
                f_store(i - 1, f_state[i - 1])

        def new_chunk_tiles():
            grouped = stage.tile([P, CHUNK_TOKENS * PACK], BF16, align_bytes=64)
            cos_t = stage.tile([P, CHUNK_TOKENS], F32)
            sin_t = stage.tile([P, CHUNK_TOKENS], F32)
            x_codes = stage.tile([P, CHUNK_TOKENS], U32, align_bytes=64)
            x_scales = stage.tile([P, CHUNK_TOKENS], U8, align_bytes=64)
            return grouped, cos_t, sin_t, x_codes, x_scales

        def new_products():
            by_cos = products.tile([P, HEADS, CHUNK_TOKENS], F32)
            by_sin = products.tile([P, HEADS, CHUNK_TOKENS], F32)
            return by_cos, by_sin

        sign = consts[:, SIGN : SIGN + 1]

        grouped_f = stage.tile([P, CHUNK_TOKENS * PACK], BF16, align_bytes=64)
        grouped, cos_t, sin_t, x_codes, x_scales = new_chunk_tiles()
        transpose_x(F_CHUNKS[0], 0, grouped_f, nc.vector.tensor_copy)
        transpose_x(F_CHUNKS[0], 2, grouped_f, nc.vector.tensor_copy)
        negate_sin(0)
        transpose_x(A_CHUNKS[0], 0, grouped, nc.scalar.copy)
        transpose_x(A_CHUNKS[0], 2, grouped, nc.scalar.copy)
        quantise(grouped_f, *f_operands[0])
        doubled_cos = double_table(A_CHUNKS[0], cos_sb)
        doubled_sin = double_table(A_CHUNKS[0], sin_sb)
        f_step(0)
        f_step(1)
        transpose_table(doubled_cos, cos_t, 1.0)
        transpose_table(doubled_sin, sin_t, sign)
        quantise(grouped, x_codes, x_scales)

        before = None
        for a in range(len(A_CHUNKS)):
            c = A_CHUNKS[a]
            more = a + 1 < len(A_CHUNKS)
            following = A_CHUNKS[a + 1] if more else None
            inputs = (x_codes, x_scales, cos_t, sin_t)
            if more:
                grouped, next_cos_t, next_sin_t, next_codes, next_scales = new_chunk_tiles()
            queries = None
            keys = None
            for q in range(4):
                step = 4 * a + q
                f_step(step + F_PERIOD)
                if q == 0:
                    queries = new_products()
                if q == 2:
                    keys = new_products()
                unit = queries if q < 2 else keys
                multiply(*unit, q // 2, 2 * (q % 2), *inputs)
                if more and q < 2:
                    transpose_x(following, 2 * q, grouped, nc.scalar.copy)
                if more and q == 2:
                    transpose_table(doubled_cos, next_cos_t, 1.0)
                    quantise(grouped, next_codes, next_scales)
                if more and q == 3:
                    transpose_table(doubled_sin, next_sin_t, sign)
                if step == 2:
                    grouped_f = stage.tile([P, CHUNK_TOKENS * PACK], BF16, align_bytes=64)
                    transpose_x(F_CHUNKS[1], 0, grouped_f, nc.scalar.copy)
                if step == 5:
                    transpose_x(F_CHUNKS[1], 2, grouped_f, nc.scalar.copy)
                    negate_sin(1)
                if step == 6:
                    quantise(grouped_f, *f_operands[1])
                if q < 2 and before is not None:
                    turn_back(before[0], 1, 2 * q, *before[1])
                if q >= 2:
                    turn_back(c, 0, 2 * (q - 2), *queries)
                if more and q == 0:
                    doubled_cos = double_table(following, cos_sb)
                if more and q == 1:
                    doubled_sin = double_table(following, sin_sb)
            before = (c, keys)
            if more:
                x_codes, x_scales, cos_t, sin_t = next_codes, next_scales, next_cos_t, next_sin_t

        turn_back_by_heads(before[0], 1, *before[1])
